import numpy as np
import ml_dtypes


def mxq(x, axis, fmt="e4m3"):
    dtype, down = {"e4m3": (ml_dtypes.float8_e4m3fn, 7), "e5m2": (ml_dtypes.float8_e5m2, 14)}[fmt]
    v = np.moveaxis(np.asarray(x, np.float32).astype(ml_dtypes.bfloat16).astype(np.float64), axis, -1)
    blocks = v.reshape(v.shape[:-1] + (-1, 32))
    amax = np.abs(blocks).max(-1, keepdims=True)
    byte = np.maximum(np.where(amax > 0, np.frexp(amax)[1] - 1 + 127, 0) - down, 1)
    scale = np.exp2(byte - 127.0)
    codes = (blocks / scale).astype(np.float32).astype(dtype).astype(np.float64)
    return np.moveaxis((codes * scale).reshape(v.shape), -1, axis)


WIDE = False


def mx_kscale(k):
    if not WIDE:
        return np.ones(k)
    levels = np.array([10, -10, 5, -5, 0])
    if k % 512:
        return np.exp2(np.random.permutation(np.resize(levels, k // 32))).repeat(32)
    a = np.empty((k // 512, 16))
    for p in range(k // 512):
        a[p, :8] = np.random.permutation(np.resize(levels, 8))
        for g in range(8):
            far = levels[np.abs(levels - a[p, g]) >= 10]
            a[p, g + 8] = far[np.random.randint(len(far))]
    return np.exp2(a.ravel()).repeat(32)


BF16 = ml_dtypes.bfloat16


def bf(x):
    return np.asarray(x, np.float32).astype(BF16)


def f64(x):
    return np.asarray(x).astype(np.float64)


E2M1 = np.array([0.0, 0.5, 1.0, 1.5, 2.0, 3.0, 4.0, 6.0, -0.0, -0.5, -1.0, -1.5, -2.0, -3.0, -4.0, -6.0])


def pack_weight(w, fmt):
    k, n = w.shape
    w = f64(bf(w)).reshape(k // 32, 32, n)
    amax = np.abs(w).max(1)
    if fmt == "e4m3":
        byte = np.frexp(amax)[1] - 1 + 127 - 7
    else:
        mant, ex = np.frexp(amax / 6.0)
        byte = np.where(mant > 0.5, ex, ex - 1) + 127
    byte = np.clip(np.where(amax > 0, byte, 1), 1, 254)
    scaled = (w * np.exp2(127.0 - byte)[:, None, :]).reshape(k, n).astype(np.float32)
    by_word = np.ascontiguousarray(scaled.reshape(k // 512, 128, 4, n).transpose(0, 1, 3, 2))
    if fmt == "e4m3":
        words = by_word.astype(ml_dtypes.float8_e4m3fn).view(np.uint8)
    else:
        c = by_word.astype(ml_dtypes.float4_e2m1fn).view(np.uint8) & 0xF
        words = c[..., 0::2] | (c[..., 1::2] << 4)
    return np.ascontiguousarray(words), np.ascontiguousarray(byte.astype(np.uint8).reshape(k // 512, 16, n))


def unpack_weight(words, scales, fmt):
    g, p, n, _ = words.shape
    if fmt == "e4m3":
        vals = np.ascontiguousarray(words).view(ml_dtypes.float8_e4m3fn).astype(np.float64)
    else:
        nib = np.empty((g, p, n, 4), np.uint8)
        nib[..., 0::2] = words & 0xF
        nib[..., 1::2] = words >> 4
        vals = E2M1[nib]
    vals = vals * np.repeat(np.exp2(scales.astype(np.float64) - 127.0), 8, axis=1)[..., None]
    return vals.transpose(0, 1, 3, 2).reshape(g * 512, n)


B, S, E, LAT, H = 4, 2048, 512, 512, 4
D = E // H
R = D // 2
HR = H * R


def rope_cos_sin(n):
    inv_freq = 1.0 / (10000.0 ** (np.arange(0, R, 2) / R))
    freqs = np.outer(np.arange(n), inv_freq)
    emb = np.concatenate([freqs, freqs], axis=-1)
    return np.cos(emb), np.sin(emb)


def rotate_half(v):
    v1, v2 = v[..., : R // 2], v[..., R // 2 :]
    return np.concatenate([-v2, v1], axis=-1)


def apply_rope(v, cos, sin):
    return v * cos[None, :, None, :] + rotate_half(v) * sin[None, :, None, :]


def draw0():
    s, t = mx_kscale(E), mx_kscale(LAT)
    x = bf(np.random.standard_normal((B, S, E)) * s)
    Wq_d = np.random.standard_normal((LAT, E)) / np.sqrt(E) * t[:, None] / s[None, :]
    bq_d = bf(np.random.standard_normal(LAT) * 0.3 * t)
    Wq_u = np.random.standard_normal((HR, LAT)) / np.sqrt(LAT) / t[None, :]
    bq_u = bf(np.random.standard_normal(HR) * 0.3)
    Wrq = np.random.standard_normal((HR, LAT)) / np.sqrt(LAT) / t[None, :]
    brq = bf(np.random.standard_normal(HR) * 0.3)
    Wq_d_words, Wq_d_scales = pack_weight(Wq_d.T, "e4m3")
    Wq_u_words, Wq_u_scales = pack_weight(Wq_u.T, "e4m3")
    Wrq_words, Wrq_scales = pack_weight(Wrq.T, "e4m3")
    return {
        "x": x,
        "Wq_d_words": Wq_d_words,
        "Wq_d_scales": Wq_d_scales,
        "bq_d": bq_d,
        "Wq_u_words": Wq_u_words,
        "Wq_u_scales": Wq_u_scales,
        "bq_u": bq_u,
        "Wrq_words": Wrq_words,
        "Wrq_scales": Wrq_scales,
        "brq": brq,
    }


def core(x, Wq_d_words, Wq_d_scales, bq_d, Wq_u_words, Wq_u_scales, bq_u, Wrq_words, Wrq_scales, brq):
    q_d = (mxq(f64(x), 2, "e4m3") @ unpack_weight(Wq_d_words, Wq_d_scales, "e4m3")) + f64(bq_d)
    qdq = mxq(q_d, 2, "e4m3")
    q1 = ((qdq @ unpack_weight(Wq_u_words, Wq_u_scales, "e4m3")) + f64(bq_u)).reshape(B, S, H, R)
    qr = ((qdq @ unpack_weight(Wrq_words, Wrq_scales, "e4m3")) + f64(brq)).reshape(B, S, H, R)
    cos, sin = rope_cos_sin(S)
    qr = apply_rope(qr, cos, sin)
    return np.concatenate([q1, qr], axis=-1)


def e4m3fn_bytes(y):
    return np.clip(np.asarray(y, np.float64), -448.0, 448.0).astype(np.float32).astype(ml_dtypes.float8_e4m3fn).view(np.uint8)


def e4m3fn_values(b):
    return np.asarray(b, np.uint8).view(ml_dtypes.float8_e4m3fn).astype(np.float64)


def setup_inputs():
    d = draw0()
    x0 = np.asarray(d['x']).astype(np.float64)
    s = (np.max(np.abs(x0), axis=(0, 1), keepdims=True) / 448.0).astype(np.float32)
    out = {}
    for k, v in d.items():
        if k == 'x':
            out['x_bytes'] = e4m3fn_bytes(x0 / s.astype(np.float64))
            out['x_scale'] = s
        else:
            out[k] = v
    return out


def reference(x_bytes, x_scale, Wq_d_words, Wq_d_scales, bq_d, Wq_u_words, Wq_u_scales, bq_u, Wrq_words, Wrq_scales, brq):
    return core(e4m3fn_values(x_bytes) * x_scale.astype(np.float64), Wq_d_words, Wq_d_scales, bq_d, Wq_u_words, Wq_u_scales, bq_u, Wrq_words, Wrq_scales, brq)

@@ -1,0 +1,428 @@
+import math
+from contextlib import ExitStack
+
+import concourse.mybir as mybir
+from concourse.masks import make_identity
+
+B, S, E, LAT, H = 4, 2048, 512, 512, 4
+D = E // H
+R = D // 2
+HALF = R // 2
+FLOPS = 2 * B * S * LAT * (E + 2 * H * R)
+
+F32 = mybir.dt.float32
+BF16 = mybir.dt.bfloat16
+I32 = mybir.dt.int32
+U32 = mybir.dt.uint32
+U8 = mybir.dt.uint8
+FP8 = mybir.dt.float8_e4m3fn
+FP8X4 = mybir.dt.float8_e4m3fn_x4
+ALU = mybir.AluOpType
+ACT = mybir.ActivationFunctionType
+
+P = 128
+PACK = 4
+TILES = 4
+TOK = P * TILES
+QUARTERS = S // TOK
+GROUPS = B * QUARTERS
+
+
+def tile_multiheadlatentattention_pa_t_w8_kernel(
+    tc, x_bytes, x_scale, wd_words, wd_scales, bq_d, wu_words, wu_scales, bq_u, wr_words, wr_scales, brq, out
+):
+    nc = tc.nc
+    x_view = x_bytes.rearrange("b (c p i) k -> b c p (i k)", p=P, i=TILES)
+    out_view = out.rearrange("b (c p i) h d -> b c p (i h d)", p=P, i=TILES)
+
+    with ExitStack() as ctx:
+        keep = ctx.enter_context(tc.tile_pool(name="keep", bufs=1))
+        xin = ctx.enter_context(tc.tile_pool(name="xin", bufs=4))
+        mid = ctx.enter_context(tc.tile_pool(name="mid", bufs=2))
+        outs = ctx.enter_context(tc.tile_pool(name="outs", bufs=4))
+        psum_v = ctx.enter_context(tc.psum_pool(name="psum_v", bufs=3))
+        psum_s = ctx.enter_context(tc.psum_pool(name="psum_s", bufs=5))
+        ctx.enter_context(tc.manual_schedule())
+
+        def vbank():
+            t = psum_v.tile([P, 512], F32, name="vb", tag="vb")
+            return t
+
+        def sbank():
+            t = psum_s.tile([P, 512], F32, name="sb", tag="sb")
+            return t
+
+        x_tiles = {}
+
+        def load(g):
+            t = xin.tile([P, TILES * E], U8, name="xb", tag="xb", align_bytes=64)
+            nc.sync.dma_start(out=t[:], in_=x_view[g % B, g // B])
+            x_tiles[g] = t
+
+        xscale = keep.tile([P, 2 * E], F32, name="xscale")
+        nc.scalar.dma_start(out=xscale[:, 0:E], in_=x_scale.rearrange("a b k -> (a b k)").partition_broadcast(P))
+        load(0)
+        planes = keep.tile([P, 1024], U8, name="planes", align_bytes=64)
+        nc.gpsimd.memset(planes[:].bitcast(I32), 0)
+        wd_raw = keep.tile([P, LAT], I32, name="wd_raw", align_bytes=64)
+        nc.sync.dma_start(out=wd_raw[:], in_=wd_words[0].rearrange("p n t -> p (n t)").bitcast(I32))
+        for q in range(4):
+            nc.sync.dma_start(out=planes[32 * q : 32 * q + 4, 0:512].bitcast(I32), in_=wd_scales[0, 4 * q : 4 * q + 4, :].bitcast(I32))
+        load(1)
+        bd_raw = keep.tile([P, PACK], BF16, name="bd_raw")
+        nc.scalar.dma_start(out=bd_raw[:], in_=bq_d.rearrange("(p t) -> p t", t=PACK))
+        br_raw = keep.tile([2, P], BF16, name="br_raw")
+        for f in range(2):
+            nc.scalar.dma_start(
+                out=br_raw[f : f + 1, :].rearrange("o (h j) -> o h j", h=H),
+                in_=brq.rearrange("(h f j) -> f h j", f=2, j=HALF)[f : f + 1],
+            )
+        bu = keep.tile([P, H * R], BF16, name="bu")
+        nc.scalar.dma_start(out=bu[:], in_=bq_u.partition_broadcast(P))
+        wr = keep.tile([P, 256], I32, name="wr", align_bytes=64)
+        wr_src = wr_words[0].rearrange("p n t -> p (n t)").bitcast(I32).rearrange("p (h f j) -> f p h j", f=2, j=HALF)
+        for f in range(2):
+            nc.sync.dma_start(out=wr[:, 128 * f : 128 * f + 128].rearrange("p (h j) -> p h j", h=H), in_=wr_src[f])
+        wu = keep.tile([P, 256], I32, name="wu", align_bytes=64)
+        nc.sync.dma_start(out=wu[:], in_=wu_words[0].rearrange("p n t -> p (n t)").bitcast(I32))
+        for q in range(4):
+            nc.sync.dma_start(out=planes[32 * q : 32 * q + 4, 512:768].bitcast(I32), in_=wr_scales[0, 4 * q : 4 * q + 4, :].bitcast(I32))
+        for q in range(4):
+            nc.sync.dma_start(out=planes[32 * q : 32 * q + 4, 768:1024].bitcast(I32), in_=wu_scales[0, 4 * q : 4 * q + 4, :].bitcast(I32))
+        load(2)
+
+        ones = keep.tile([P, H], F32, name="ones")
+        nc.vector.memset(ones[:], 1.0)
+        seed = keep.tile([P, P], F32, name="seed")
+        nc.vector.memset(seed[:], 0.0)
+        brow = keep.tile([P, P], F32, name="brow")
+        nc.gpsimd.memset(brow[:], 0.0)
+        ident = keep.tile([P, P], F32, name="ident")
+        make_identity(nc, ident[:])
+
+        for j in range(HALF):
+            w1 = 10000.0 ** (-j / HALF)
+            w32 = 32.0 * w1
+
+            def put_v(row, value):
+                nc.vector.tensor_scalar(out=seed[row : row + 1, j:P:HALF], in0=ones[row : row + 1, :], scalar1=value, scalar2=None, op0=ALU.mult)
+
+            def put_s(row, value):
+                nc.scalar.mul(seed[row : row + 1, j:P:HALF], ones[row : row + 1, :], value)
+
+            def put_g(row, value):
+                nc.gpsimd.tensor_scalar(out=seed[row : row + 1, j:P:HALF], in0=ones[row : row + 1, :], scalar1=value, scalar2=0.0, op0=ALU.mult, op1=ALU.add)
+
+            put_v(0, math.cos(w1))
+            (put_s if j < 8 else put_g)(32, math.sin(w1))
+            put_s(64, math.cos(w32))
+            put_v(96, math.sin(w32))
+
+        NW = 11
+        ce = keep.tile([P, NW], F32, name="ce")
+        se = keep.tile([P, NW], F32, name="se")
+        sc = keep.tile([P, NW], F32, name="sc")
+        tmp = keep.tile([P, 2], F32, name="tmp")
+        bias_r = keep.tile([P, 3], F32, name="bias_r")
+        bias_d = keep.tile([P, PACK], F32, name="bias_d")
+
+        def columns():
+            ct = sbank()
+            nc.tensor.transpose(ct[:, 0:128], seed[:], ident[:])
+            nc.tensor.transpose(ct[:, 128:256], brow[:], ident[:])
+            nc.vector.tensor_copy(out=ce[:, 0:6:5], in_=ct[:, 0:128:64])
+            nc.vector.tensor_copy(out=se[:, 0:6:5], in_=ct[:, 32:128:64])
+            nc.vector.tensor_copy(out=bias_r[:, 0:2], in_=ct[:, 128:130])
+            nc.vector.tensor_add(bias_r[:, 2:3], bias_r[:, 0:1], bias_r[:, 1:2])
+            nc.vector.tensor_copy(out=bias_d[:], in_=bd_raw[:])
+
+        tab_c = keep.tile([P, S], F32, name="tab_c")
+        tab_u = keep.tile([P, S], F32, name="tab_u")
+        tab_w = keep.tile([P, S], F32, name="tab_w")
+        prod = keep.tile([P, 2, S // 2], F32, name="prod")
+        nc.vector.memset(tab_c[:, 0:1], 1.0)
+        nc.vector.memset(tab_u[:, 0:1], -1.0)
+        nc.vector.memset(tab_w[:, 0:1], -1.0)
+
+        tiny = []
+
+        def drip(n):
+            for f in tiny[:n]:
+                f()
+            tiny[:] = tiny[n:]
+
+        def squares():
+            for r in range(5):
+                a = slice(r, r + 6, 5) if r < 4 else slice(9, 10)
+                b = slice(r + 1, r + 7, 5) if r < 4 else slice(10, 11)
+                n = 2 if r < 4 else 1
+
+                def square(a=a, b=b, n=n):
+                    nc.vector.scalar_tensor_tensor(out=tmp[:, 0:n], in0=se[:, a], scalar=-2.0, in1=se[:, a], op0=ALU.mult, op1=ALU.mult)
+                    nc.vector.scalar_tensor_tensor(out=se[:, b], in0=se[:, a], scalar=2.0, in1=ce[:, a], op0=ALU.mult, op1=ALU.mult)
+                    nc.vector.tensor_scalar(out=ce[:, b], in0=tmp[:, 0:n], scalar1=1.0, scalar2=None, op0=ALU.add)
+
+                tiny.append(square)
+            tiny.append(lambda: nc.vector.tensor_add(sc[:], ce[:], se[:]))
+
+        def products(n0, w, lo, hi, on_scalar):
+            for t, tab in ((0, tab_w), (1, tab_u)):
+                if on_scalar:
+                    nc.scalar.activation(out=prod[:, t, 0 : hi - lo], in_=tab[:, lo:hi], func=ACT.Copy, scale=se[:, w : w + 1])
+                else:
+                    nc.vector.tensor_scalar(out=prod[:, t, 0 : hi - lo], in0=tab[:, lo:hi], scalar1=se[:, w : w + 1], scalar2=None, op0=ALU.mult)
+
+        def rotate(which, n0, w, lo, hi):
+            tab, coef, t, op = (
+                (tab_u, ce, 0, ALU.add),
+                (tab_w, ce, 1, ALU.subtract),
+                (tab_c, sc, 1, ALU.add),
+            )[which]
+            nc.vector.scalar_tensor_tensor(
+                out=tab[:, n0 + lo : n0 + hi], in0=tab[:, lo:hi], scalar=coef[:, w : w + 1], in1=prod[:, t, 0 : hi - lo], op0=ALU.mult, op1=op
+            )
+
+        level_weights = (2, 3, 4, 5, 6, 7, 8, 0, 1)
+
+        def level(k):
+            n = 1 << k
+            tiny.append(lambda: products(n, level_weights[k], 0, n, n >= 128))
+
+            def turn_all():
+                for which in range(3):
+                    rotate(which, n, level_weights[k], 0, n)
+
+            tiny.append(turn_all)
+
+        wd = keep.tile([P, LAT], I32, name="wd", align_bytes=64)
+        wds = keep.tile([P, LAT], U8, name="wds", align_bytes=64)
+        wrs = keep.tile([P, 256], U8, name="wrs", align_bytes=64)
+        wus = planes[:, 768:1024]
+
+        def permute_weights():
+            nc.vector.tensor_copy(out=wd[:].rearrange("p (t m) -> p t m", t=PACK), in_=wd_raw[:].rearrange("p (m t) -> p t m", t=PACK))
+            nc.vector.tensor_copy(out=wds[:].rearrange("p (t m) -> p t m", t=PACK), in_=planes[:, 0:512].rearrange("p (m t) -> p t m", t=PACK))
+            nc.vector.tensor_copy(
+                out=wrs[:].rearrange("p (f h j) -> p f h j", f=2, h=H), in_=planes[:, 512:768].rearrange("p (h f j) -> p f h j", f=2, h=H)
+            )
+
+        st = {}
+
+        def widen(g, tiles):
+            if g >= GROUPS:
+                return
+            if ("xs", g) not in st:
+                xs_t = mid.tile([P, TILES, E], BF16, name="xs", tag="xs", align_bytes=64)
+                st["xs", g] = xs_t
+            xs = st["xs", g]
+            step = 1 if g == 0 else 2
+            for i in tiles[::step]:
+                nc.vector.tensor_tensor(
+                    out=xs[:, i : i + step, :].rearrange("p i k -> p (i k)"),
+                    in0=x_tiles[g][:, E * i : E * (i + step)].bitcast(FP8),
+                    in1=xscale[:, 0 : E * step],
+                    op=ALU.mult,
+                )
+
+        def turn(g, pair):
+            if g >= GROUPS:
+                return
+            if ("xg", g) not in st:
+                xg_t = mid.tile([P, TOK, PACK], BF16, name="xg", tag="xg", align_bytes=64)
+                st["xg", g] = xg_t
+            bank = sbank()
+            for i in (0, 1):
+                words = st["xs", g][:, 2 * pair + i, :].bitcast(F32)
+                for u in (0, 1):
+                    o = 256 * i + 128 * u
+                    nc.tensor.transpose(bank[:, o : o + 128], words[:, u:256:2], ident[:])
+            st["xt", g, pair] = bank
+
+        def unturn(g, pair):
+            if g >= GROUPS:
+                return
+            nc.scalar.copy(
+                out=st["xg", g][:, 256 * pair : 256 * pair + 256, :].rearrange("p n t -> p (n t)").bitcast(F32).rearrange("p (i r u) -> p i r u", i=2, u=2),
+                in_=st["xt", g, pair][:].rearrange("p (i u r) -> p i r u", i=2, u=2),
+            )
+
+        def quant(src, dst, g):
+            codes = mid.tile([P, TOK], U32, name=dst, tag=dst, align_bytes=64)
+            scales = mid.tile([P, TOK], U8, name=dst + "s", tag=dst + "s", align_bytes=64)
+            nc.vector.quantize_mx(out=codes[:].bitcast(FP8X4), scales=scales[:], in_=st[src, g][:].rearrange("p n t -> p (n t)"))
+            st[dst, g] = (codes, scales)
+
+        def mm1(g):
+            codes, scales = st["xq", g]
+            for t in range(PACK):
+                bank = sbank()
+                nc.tensor.matmul_mx(
+                    out=bank[:],
+                    lhsT=wd[:, 128 * t : 128 * t + 128].bitcast(FP8X4),
+                    lhsT_scale=wds[:, 128 * t : 128 * t + 128],
+                    rhs=codes[:].bitcast(FP8X4),
+                    rhs_scale=scales[:],
+                    start=True,
+                    stop=True,
+                )
+                st["m1", g, t] = bank
+
+        def latent(g):
+            dp = mid.tile([P, PACK, TOK], BF16, name="dp", tag="dp", align_bytes=64)
+            for t in range(PACK):
+                nc.scalar.activation(out=dp[:, t, :], in_=st["m1", g, t][:], func=ACT.Identity, bias=bias_d[:, t : t + 1])
+            st["dp", g] = dp
+
+        def weave(g):
+            dg = mid.tile([P, TOK, PACK], BF16, name="dg", tag="dg", align_bytes=64)
+            for n0 in range(0, TOK, 256):
+                nc.gpsimd.tensor_scalar(
+                    out=dg[:, n0 : n0 + 256, :],
+                    in0=st["dp", g][:, :, n0 : n0 + 256].rearrange("p t n -> p n t"),
+                    scalar1=1.0,
+                    scalar2=0.0,
+                    op0=ALU.mult,
+                    op1=ALU.add,
+                )
+            st["dg", g] = dg
+
+        def mm_rope(g, parts):
+            codes, scales = st["dq", g]
+            bank = vbank()
+            for n, f in enumerate(parts):
+                nc.tensor.matmul_mx(
+                    out=bank[:],
+                    lhsT=wr[:, 128 * f : 128 * f + 128].bitcast(FP8X4),
+                    lhsT_scale=wrs[:, 128 * f : 128 * f + 128],
+                    rhs=codes[:].bitcast(FP8X4),
+                    rhs_scale=scales[:],
+                    start=(n == 0),
+                    stop=(n == len(parts) - 1),
+                )
+            st["k", g, parts] = bank
+
+        def mm_q1(g, pair):
+            codes, scales = st["dq", g]
+            bank = vbank()
+            for i in (0, 1):
+                c0 = 256 * pair + 128 * i
+                nc.tensor.matmul_mx(
+                    out=bank[:, 256 * i : 256 * i + 256],
+                    lhsT=codes[:, c0 : c0 + 128].bitcast(FP8X4),
+                    lhsT_scale=scales[:, c0 : c0 + 128],
+                    rhs=wu[:].bitcast(FP8X4),
+                    rhs_scale=wus,
+                    start=True,
+                    stop=True,
+                )
+            st["q1", g, pair] = bank
+
+        SUM, HI, LO = (0, 1), (1,), (0,)
+
+        def rope(g, parts):
+            bias_col, tab = {SUM: (2, tab_c), HI: (1, tab_u), LO: (0, tab_w)}[parts]
+            c0 = (g // B) * TOK
+            kt = mid.tile([P, TOK], F32, name="kt", tag="k%d" % bias_col)
+            nc.vector.scalar_tensor_tensor(
+                out=kt[:], in0=st["k", g, parts][:], scalar=bias_r[:, bias_col : bias_col + 1], in1=tab[:, c0 : c0 + TOK], op0=ALU.add, op1=ALU.mult
+            )
+            st["kt", g, parts] = kt
+
+        def finish_q1(g, pair):
+            if ("ot", g) not in st:
+                ot_t = outs.tile([P, TILES, H, D], F32, name="ot", tag="ot")
+                st["ot", g] = ot_t
+            nc.vector.tensor_tensor(
+                out=st["ot", g][:, 2 * pair : 2 * pair + 2, :, 0:R],
+                in0=st["q1", g, pair][:].rearrange("p (i h d) -> p i h d", i=2, h=H),
+                in1=bu[:].rearrange("p (o h d) -> p o h d", o=1, h=H).to_broadcast([P, 2, H, R]),
+                op=ALU.add,
+            )
+
+        def back(g, half):
+            bank = sbank()
+            pieces = (SUM, HI) if half == 0 else (SUM, LO)
+            for i in range(TILES):
+                for n, parts in enumerate(pieces):
+                    nc.tensor.matmul(
+                        bank[:, 128 * i : 128 * i + 128],
+                        st["kt", g, parts][:, 128 * i : 128 * i + 128],
+                        ident[:],
+                        start=(n == 0),
+                        stop=(n == 1),
+                        is_transpose=True,
+                    )
+            st["o", g, half] = bank
+
+        def place(g, half):
+            c0 = R + HALF * half
+            nc.scalar.copy(
+                out=st["ot", g][:, :, :, c0 : c0 + HALF],
+                in_=st["o", g, half][:].rearrange("p (i h j) -> p i h j", i=TILES, h=H),
+            )
+
+        def store(g):
+            nc.sync.dma_start(out=out_view[g % B, g // B], in_=st["ot", g][:].rearrange("p i h d -> p (i h d)"))
+
+        nc.vector.tensor_copy(out=brow[0:2, :], in_=br_raw[:])
+        widen(0, (0, 1))
+        turn(0, 0)
+        unturn(0, 0)
+        widen(0, (2, 3))
+        turn(0, 1)
+        unturn(0, 1)
+        nc.scalar.copy(out=xscale[:, E : 2 * E], in_=xscale[:, 0:E])
+        permute_weights()
+        columns()
+        squares()
+        for k in range(9):
+            level(k)
+        drip(2)
+
+        for i in range(GROUPS + 2):
+            if i + 3 < GROUPS:
+                load(i + 3)
+            a, b, c = i - 2, i - 1, i
+            if 0 <= b < GROUPS:
+                weave(b)
+            if a >= 0:
+                rope(a, SUM)
+                mm_q1(a, 1)
+                finish_q1(a, 0)
+                mm_rope(a, LO)
+                rope(a, HI)
+                back(a, 0)
+                place(a, 0)
+                finish_q1(a, 1)
+                rope(a, LO)
+                back(a, 1)
+                place(a, 1)
+                store(a)
+            if 3 <= i <= 5:
+                if i == 3:
+                    products(512, 9, 0, 512, True)
+                rotate(i - 3, 512, 9, 0, 512)
+            if i in (6, 7, 8, 10, 11, 12):
+                lo = 0 if i < 9 else 512
+                if i in (6, 10):
+                    products(1024, 10, lo, lo + 512, True)
+                rotate((i - 6) % 4, 1024, 10, lo, lo + 512)
+            if c < GROUPS:
+                quant("xg", "xq", c)
+                mm1(c)
+                latent(c)
+            drip(4)
+            widen(c + 1, (0, 1))
+            drip(4)
+            turn(c + 1, 0)
+            unturn(c + 1, 0)
+            if 0 <= b < GROUPS:
+                quant("dg", "dq", b)
+                mm_rope(b, SUM)
+                mm_q1(b, 0)
+                mm_rope(b, HI)
+            drip(4)
+            widen(c + 1, (2, 3))
+            drip(3)
+            turn(c + 1, 1)
+            unturn(c + 1, 1)

@@ -26,6 +26,8 @@ TILES = 4
 TOK = P * TILES
 QUARTERS = S // TOK
 GROUPS = B * QUARTERS
+SPLIT = 256
+DUMMIES = (0, 1, 0, 1)
 
 
 def tile_multiheadlatentattention_pa_t_w8_kernel(
@@ -37,7 +39,7 @@ def tile_multiheadlatentattention_pa_t_w8_kernel(
 
     with ExitStack() as ctx:
         keep = ctx.enter_context(tc.tile_pool(name="keep", bufs=1))
-        xin = ctx.enter_context(tc.tile_pool(name="xin", bufs=4))
+        xin = ctx.enter_context(tc.tile_pool(name="xin", bufs=5))
         mid = ctx.enter_context(tc.tile_pool(name="mid", bufs=2))
         outs = ctx.enter_context(tc.tile_pool(name="outs", bufs=4))
         psum_v = ctx.enter_context(tc.psum_pool(name="psum_v", bufs=3))
@@ -53,6 +55,10 @@ def tile_multiheadlatentattention_pa_t_w8_kernel(
             return t
 
         x_tiles = {}
+
+        def warm(bank, n):
+            for k in range(n):
+                nc.tensor.matmul(bank[:, 0:128], ident[:], ident[:], start=True, stop=True)
 
         def load(g):
             t = xin.tile([P, TILES * E], U8, name="xb", tag="xb", align_bytes=64)
@@ -90,6 +96,7 @@ def tile_multiheadlatentattention_pa_t_w8_kernel(
         for q in range(4):
             nc.sync.dma_start(out=planes[32 * q : 32 * q + 4, 768:1024].bitcast(I32), in_=wu_scales[0, 4 * q : 4 * q + 4, :].bitcast(I32))
         load(2)
+        load(3)
 
         ones = keep.tile([P, H], F32, name="ones")
         nc.vector.memset(ones[:], 1.0)
@@ -128,6 +135,7 @@ def tile_multiheadlatentattention_pa_t_w8_kernel(
 
         def columns():
             ct = sbank()
+            nc.vector.tensor_copy(out=brow[0:2, :], in_=br_raw[:])
             nc.tensor.transpose(ct[:, 0:128], seed[:], ident[:])
             nc.tensor.transpose(ct[:, 128:256], brow[:], ident[:])
             nc.vector.tensor_copy(out=ce[:, 0:6:5], in_=ct[:, 0:128:64])
@@ -165,28 +173,28 @@ def tile_multiheadlatentattention_pa_t_w8_kernel(
                 tiny.append(square)
             tiny.append(lambda: nc.vector.tensor_add(sc[:], ce[:], se[:]))
 
-        def products(n0, w, lo, hi, on_scalar):
+        def products(n0, w, lo, hi, on_scalar, base=0):
             for t, tab in ((0, tab_w), (1, tab_u)):
                 if on_scalar:
-                    nc.scalar.activation(out=prod[:, t, 0 : hi - lo], in_=tab[:, lo:hi], func=ACT.Copy, scale=se[:, w : w + 1])
+                    nc.scalar.activation(out=prod[:, t, base : base + hi - lo], in_=tab[:, lo:hi], func=ACT.Copy, scale=se[:, w : w + 1])
                 else:
                     nc.vector.tensor_scalar(out=prod[:, t, 0 : hi - lo], in0=tab[:, lo:hi], scalar1=se[:, w : w + 1], scalar2=None, op0=ALU.mult)
 
-        def rotate(which, n0, w, lo, hi):
+        def rotate(which, n0, w, lo, hi, base=0):
             tab, coef, t, op = (
                 (tab_u, ce, 0, ALU.add),
                 (tab_w, ce, 1, ALU.subtract),
                 (tab_c, sc, 1, ALU.add),
             )[which]
             nc.vector.scalar_tensor_tensor(
-                out=tab[:, n0 + lo : n0 + hi], in0=tab[:, lo:hi], scalar=coef[:, w : w + 1], in1=prod[:, t, 0 : hi - lo], op0=ALU.mult, op1=op
+                out=tab[:, n0 + lo : n0 + hi], in0=tab[:, lo:hi], scalar=coef[:, w : w + 1], in1=prod[:, t, base : base + hi - lo], op0=ALU.mult, op1=op
             )
 
         level_weights = (2, 3, 4, 5, 6, 7, 8, 0, 1)
 
         def level(k):
             n = 1 << k
-            tiny.append(lambda: products(n, level_weights[k], 0, n, n >= 128))
+            tiny.append(lambda: products(n, level_weights[k], 0, n, False))
 
             def turn_all():
                 for which in range(3):
@@ -231,6 +239,7 @@ def tile_multiheadlatentattention_pa_t_w8_kernel(
                 xg_t = mid.tile([P, TOK, PACK], BF16, name="xg", tag="xg", align_bytes=64)
                 st["xg", g] = xg_t
             bank = sbank()
+            warm(bank, DUMMIES[2 + pair])
             for i in (0, 1):
                 words = st["xs", g][:, 2 * pair + i, :].bitcast(F32)
                 for u in (0, 1):
@@ -268,23 +277,32 @@ def tile_multiheadlatentattention_pa_t_w8_kernel(
                 st["m1", g, t] = bank
 
         def latent(g):
-            dp = mid.tile([P, PACK, TOK], BF16, name="dp", tag="dp", align_bytes=64)
+            dp = mid.tile([P, PACK, SPLIT], BF16, name="dp", tag="dp", align_bytes=64)
+            dw = mid.tile([P, 2, TOK - SPLIT, 2], BF16, name="dw", tag="dw", align_bytes=64)
             for t in range(PACK):
-                nc.scalar.activation(out=dp[:, t, :], in_=st["m1", g, t][:], func=ACT.Identity, bias=bias_d[:, t : t + 1])
+                bank = st["m1", g, t]
+                nc.scalar.activation(out=dw[:, t // 2, :, t % 2], in_=bank[:, SPLIT:TOK], func=ACT.Identity, bias=bias_d[:, t : t + 1])
+                nc.scalar.activation(out=dp[:, t, :], in_=bank[:, 0:SPLIT], func=ACT.Identity, bias=bias_d[:, t : t + 1])
             st["dp", g] = dp
+            st["dw", g] = dw
 
         def weave(g):
             dg = mid.tile([P, TOK, PACK], BF16, name="dg", tag="dg", align_bytes=64)
-            for n0 in range(0, TOK, 256):
-                nc.gpsimd.tensor_scalar(
-                    out=dg[:, n0 : n0 + 256, :],
-                    in0=st["dp", g][:, :, n0 : n0 + 256].rearrange("p t n -> p n t"),
-                    scalar1=1.0,
-                    scalar2=0.0,
-                    op0=ALU.mult,
-                    op1=ALU.add,
-                )
+            nc.gpsimd.tensor_scalar(
+                out=dg[:, 0:SPLIT, :],
+                in0=st["dp", g][:].rearrange("p t n -> p n t"),
+                scalar1=1.0,
+                scalar2=0.0,
+                op0=ALU.mult,
+                op1=ALU.add,
+            )
             st["dg", g] = dg
+
+        def weave_high(g):
+            nc.scalar.copy(
+                out=st["dg", g][:, SPLIT:TOK, :].rearrange("p n t -> p (n t)").bitcast(F32).rearrange("p (n u) -> p n u", u=2),
+                in_=st["dw", g][:].rearrange("p u n e -> p (u n e)").bitcast(F32).rearrange("p (u n) -> p n u", u=2),
+            )
 
         def mm_rope(g, parts):
             codes, scales = st["dq", g]
@@ -329,9 +347,6 @@ def tile_multiheadlatentattention_pa_t_w8_kernel(
             st["kt", g, parts] = kt
 
         def finish_q1(g, pair):
-            if ("ot", g) not in st:
-                ot_t = outs.tile([P, TILES, H, D], F32, name="ot", tag="ot")
-                st["ot", g] = ot_t
             nc.vector.tensor_tensor(
                 out=st["ot", g][:, 2 * pair : 2 * pair + 2, :, 0:R],
                 in0=st["q1", g, pair][:].rearrange("p (i h d) -> p i h d", i=2, h=H),
@@ -341,15 +356,16 @@ def tile_multiheadlatentattention_pa_t_w8_kernel(
 
         def back(g, half):
             bank = sbank()
-            pieces = (SUM, HI) if half == 0 else (SUM, LO)
+            pieces = (st["kt", g, SUM], st["kt", g, HI if half == 0 else LO])
+            warm(bank, DUMMIES[half])
             for i in range(TILES):
-                for n, parts in enumerate(pieces):
+                for n, piece in enumerate(pieces):
                     nc.tensor.matmul(
                         bank[:, 128 * i : 128 * i + 128],
-                        st["kt", g, parts][:, 128 * i : 128 * i + 128],
+                        piece[:, 128 * i : 128 * i + 128],
                         ident[:],
                         start=(n == 0),
-                        stop=(n == 1),
+                        stop=(n == len(pieces) - 1),
                         is_transpose=True,
                     )
             st["o", g, half] = bank
@@ -364,65 +380,71 @@ def tile_multiheadlatentattention_pa_t_w8_kernel(
         def store(g):
             nc.sync.dma_start(out=out_view[g % B, g // B], in_=st["ot", g][:].rearrange("p i h d -> p (i h d)"))
 
-        nc.vector.tensor_copy(out=brow[0:2, :], in_=br_raw[:])
-        widen(0, (0, 1))
-        turn(0, 0)
-        unturn(0, 0)
-        widen(0, (2, 3))
-        turn(0, 1)
-        unturn(0, 1)
-        nc.scalar.copy(out=xscale[:, E : 2 * E], in_=xscale[:, 0:E])
-        permute_weights()
-        columns()
-        squares()
-        for k in range(9):
-            level(k)
-        drip(2)
+        for g in (0, 1):
+            for pair in (0, 1):
+                widen(g, (2 * pair, 2 * pair + 1))
+                turn(g, pair)
+                if g == 0:
+                    unturn(g, pair)
+            if g == 0:
+                nc.scalar.copy(out=xscale[:, E : 2 * E], in_=xscale[:, 0:E])
+                permute_weights()
+                columns()
+                squares()
+                for k in range(9):
+                    level(k)
+                drip(2)
 
         for i in range(GROUPS + 2):
-            if i + 3 < GROUPS:
-                load(i + 3)
+            if i + 4 < GROUPS:
+                load(i + 4)
             a, b, c = i - 2, i - 1, i
+            for pair in (0, 1):
+                if c + 1 < GROUPS:
+                    unturn(c + 1, pair)
             if 0 <= b < GROUPS:
                 weave(b)
+                weave_high(b)
+            if i == 2:
+                products(512, 9, 0, 512, True)
+            if i == 6:
+                products(1024, 10, 0, 512, True, 512)
+            if i == 10:
+                products(1024, 10, 512, 1024, True)
             if a >= 0:
+                ot_t = outs.tile([P, TILES, H, D], F32, name="ot", tag="ot")
+                st["ot", a] = ot_t
                 rope(a, SUM)
-                mm_q1(a, 1)
-                finish_q1(a, 0)
-                mm_rope(a, LO)
                 rope(a, HI)
+                rope(a, LO)
+                mm_q1(a, 0)
+                mm_q1(a, 1)
                 back(a, 0)
                 place(a, 0)
-                finish_q1(a, 1)
-                rope(a, LO)
                 back(a, 1)
                 place(a, 1)
-                store(a)
-            if 3 <= i <= 5:
-                if i == 3:
-                    products(512, 9, 0, 512, True)
-                rotate(i - 3, 512, 9, 0, 512)
-            if i in (6, 7, 8, 10, 11, 12):
-                lo = 0 if i < 9 else 512
-                if i in (6, 10):
-                    products(1024, 10, lo, lo + 512, True)
-                rotate((i - 6) % 4, 1024, 10, lo, lo + 512)
             if c < GROUPS:
                 quant("xg", "xq", c)
                 mm1(c)
                 latent(c)
             drip(4)
-            widen(c + 1, (0, 1))
+            if a >= 0:
+                finish_q1(a, 0)
+                finish_q1(a, 1)
+                store(a)
+            if 3 <= i <= 5:
+                rotate(i - 3, 512, 9, 0, 512)
+            if 7 <= i <= 9:
+                rotate(i - 7, 1024, 10, 0, 512, 512)
+            if 11 <= i <= 13:
+                rotate(i - 11, 1024, 10, 512, 1024)
             drip(4)
-            turn(c + 1, 0)
-            unturn(c + 1, 0)
             if 0 <= b < GROUPS:
                 quant("dg", "dq", b)
                 mm_rope(b, SUM)
-                mm_q1(b, 0)
                 mm_rope(b, HI)
-            drip(4)
-            widen(c + 1, (2, 3))
-            drip(3)
-            turn(c + 1, 1)
-            unturn(c + 1, 1)
+                mm_rope(b, LO)
+            for pair in (0, 1):
+                drip(4)
+                widen(c + 2, (2 * pair, 2 * pair + 1))
+                turn(c + 2, pair)

@@ -69,22 +69,22 @@ def tile_multiheadlatentattention_pa_t_w8_kernel(
         nc.scalar.dma_start(out=xscale[:, 0:E], in_=x_scale.rearrange("a b k -> (a b k)").partition_broadcast(P))
         load(0)
         planes = keep.tile([P, 1024], U8, name="planes", align_bytes=64)
-        nc.gpsimd.memset(planes[:].bitcast(I32), 0)
+        nc.vector.memset(planes[:].bitcast(I32), 0)
         wd_raw = keep.tile([P, LAT], I32, name="wd_raw", align_bytes=64)
         nc.sync.dma_start(out=wd_raw[:], in_=wd_words[0].rearrange("p n t -> p (n t)").bitcast(I32))
         for q in range(4):
             nc.sync.dma_start(out=planes[32 * q : 32 * q + 4, 0:512].bitcast(I32), in_=wd_scales[0, 4 * q : 4 * q + 4, :].bitcast(I32))
         load(1)
         bd_raw = keep.tile([P, PACK], BF16, name="bd_raw")
-        nc.scalar.dma_start(out=bd_raw[:], in_=bq_d.rearrange("(p t) -> p t", t=PACK))
+        nc.sync.dma_start(out=bd_raw[:], in_=bq_d.rearrange("(p t) -> p t", t=PACK))
         br_raw = keep.tile([2, P], BF16, name="br_raw")
         for f in range(2):
-            nc.scalar.dma_start(
+            nc.sync.dma_start(
                 out=br_raw[f : f + 1, :].rearrange("o (h j) -> o h j", h=H),
                 in_=brq.rearrange("(h f j) -> f h j", f=2, j=HALF)[f : f + 1],
             )
         bu = keep.tile([P, H * R], BF16, name="bu")
-        nc.scalar.dma_start(out=bu[:], in_=bq_u.partition_broadcast(P))
+        nc.sync.dma_start(out=bu[:], in_=bq_u.partition_broadcast(P))
         wr = keep.tile([P, 256], I32, name="wr", align_bytes=64)
         wr_src = wr_words[0].rearrange("p n t -> p (n t)").bitcast(I32).rearrange("p (h f j) -> f p h j", f=2, j=HALF)
         for f in range(2):
@@ -102,114 +102,86 @@ def tile_multiheadlatentattention_pa_t_w8_kernel(
         nc.vector.memset(ones[:], 1.0)
         seed = keep.tile([P, P], F32, name="seed")
         nc.vector.memset(seed[:], 0.0)
-        brow = keep.tile([P, P], F32, name="brow")
-        nc.gpsimd.memset(brow[:], 0.0)
         ident = keep.tile([P, P], F32, name="ident")
         make_identity(nc, ident[:])
-
+        pos = keep.tile([P, TOK], F32, name="pos")
+        for c in range(QUARTERS):
+            nc.gpsimd.iota(
+                pos[32 * c : 32 * c + 32, :].rearrange("p (i m) -> p i m", i=TILES),
+                pattern=[[1, TILES], [TILES, P]],
+                base=TOK * c,
+                channel_multiplier=0,
+                allow_small_or_imprecise_dtypes=True,
+            )
+        brow = keep.tile([P, P], F32, name="brow")
+        nc.gpsimd.memset(brow[:], 0.0)
         for j in range(HALF):
-            w1 = 10000.0 ** (-j / HALF)
-            w32 = 32.0 * w1
+            turns = 10000.0 ** (-j / HALF) / (2.0 * math.pi)
+            dst, src = seed[0:1, j:P:HALF], ones[0:1, :]
+            if j < 24:
+                nc.vector.tensor_scalar(out=dst, in0=src, scalar1=turns, scalar2=None, op0=ALU.mult)
+            else:
+                nc.scalar.mul(dst, src, turns)
 
-            def put_v(row, value):
-                nc.vector.tensor_scalar(out=seed[row : row + 1, j:P:HALF], in0=ones[row : row + 1, :], scalar1=value, scalar2=None, op0=ALU.mult)
-
-            def put_s(row, value):
-                nc.scalar.mul(seed[row : row + 1, j:P:HALF], ones[row : row + 1, :], value)
-
-            def put_g(row, value):
-                nc.gpsimd.tensor_scalar(out=seed[row : row + 1, j:P:HALF], in0=ones[row : row + 1, :], scalar1=value, scalar2=0.0, op0=ALU.mult, op1=ALU.add)
-
-            put_v(0, math.cos(w1))
-            (put_s if j < 8 else put_g)(32, math.sin(w1))
-            put_s(64, math.cos(w32))
-            put_v(96, math.sin(w32))
-
-        NW = 11
-        ce = keep.tile([P, NW], F32, name="ce")
-        se = keep.tile([P, NW], F32, name="se")
-        sc = keep.tile([P, NW], F32, name="sc")
-        tmp = keep.tile([P, 2], F32, name="tmp")
+        freq = keep.tile([P, 1], F32, name="freq")
         bias_r = keep.tile([P, 3], F32, name="bias_r")
         bias_d = keep.tile([P, PACK], F32, name="bias_d")
+        angle = keep.tile([P, 2, TOK], F32, name="angle")
+        whole = keep.tile([P, 2, TOK], I32, name="whole")
+        sine = keep.tile([P, TOK], F32, name="sine")
+        trio = keep.tile([P, 3, TOK], F32, name="trio")
+        tab = keep.tile([P, 3, S], F32, name="tab")
+
+        def table_a():
+            ct = sbank()
+            nc.tensor.transpose(ct[:, 0:128], seed[:], ident[:])
+            nc.vector.tensor_copy(out=freq[:], in_=ct[:, 0:1])
+            warm(ct, 4)
+            for q in range(2):
+                nc.scalar.activation(out=angle[:, q, :], in_=pos[:], func=ACT.Copy, scale=freq[:], bias=0.25 * q)
+
+        def table_b():
+            nc.vector.tensor_copy(out=whole[:].rearrange("p q n -> p (q n)"), in_=angle[:].rearrange("p q n -> p (q n)"))
+
+        def table_c():
+            nc.vector.tensor_tensor(
+                out=angle[:].rearrange("p q n -> p (q n)"),
+                in0=angle[:].rearrange("p q n -> p (q n)"),
+                in1=whole[:].rearrange("p q n -> p (q n)"),
+                op=ALU.subtract,
+            )
+            nc.scalar.activation(out=sine[:], in_=angle[:, 0, :], func=ACT.Sin, scale=2.0 * math.pi)
+            nc.scalar.activation(out=trio[:, 0, :], in_=angle[:, 1, :], func=ACT.Sin, scale=2.0 * math.pi)
+
+        def table_d():
+            nc.vector.scalar_tensor_tensor(out=trio[:, 1, :], in0=trio[:, 0, :], scalar=-1.0, in1=sine[:], op0=ALU.mult, op1=ALU.subtract)
+            nc.vector.tensor_tensor(out=trio[:, 2, :], in0=sine[:], in1=trio[:, 0, :], op=ALU.subtract)
+            park = out_view[B - 1, QUARTERS - 1][:, 0 : 3 * TOK]
+            nc.sync.dma_start(out=park, in_=trio[:].rearrange("p t n -> p (t n)"))
+            for c in range(QUARTERS):
+                for h in range(H):
+                    nc.sync.dma_start(
+                        out=tab[32 * h : 32 * h + 32, :, TOK * c : TOK * (c + 1)], in_=park[32 * c : 32 * c + 32, :].rearrange("p (t n) -> p t n", t=3)
+                    )
 
         def columns():
             ct = sbank()
             nc.vector.tensor_copy(out=brow[0:2, :], in_=br_raw[:])
-            nc.tensor.transpose(ct[:, 0:128], seed[:], ident[:])
-            nc.tensor.transpose(ct[:, 128:256], brow[:], ident[:])
-            nc.vector.tensor_copy(out=ce[:, 0:6:5], in_=ct[:, 0:128:64])
-            nc.vector.tensor_copy(out=se[:, 0:6:5], in_=ct[:, 32:128:64])
-            nc.vector.tensor_copy(out=bias_r[:, 0:2], in_=ct[:, 128:130])
+            nc.tensor.transpose(ct[:, 0:128], brow[:], ident[:])
+            nc.vector.tensor_copy(out=bias_r[:, 0:2], in_=ct[:, 0:2])
             nc.vector.tensor_add(bias_r[:, 2:3], bias_r[:, 0:1], bias_r[:, 1:2])
             nc.vector.tensor_copy(out=bias_d[:], in_=bd_raw[:])
-
-        tab_c = keep.tile([P, S], F32, name="tab_c")
-        tab_u = keep.tile([P, S], F32, name="tab_u")
-        tab_w = keep.tile([P, S], F32, name="tab_w")
-        prod = keep.tile([P, 2, S // 2], F32, name="prod")
-        nc.vector.memset(tab_c[:, 0:1], 1.0)
-        nc.vector.memset(tab_u[:, 0:1], -1.0)
-        nc.vector.memset(tab_w[:, 0:1], -1.0)
-
-        tiny = []
-
-        def drip(n):
-            for f in tiny[:n]:
-                f()
-            tiny[:] = tiny[n:]
-
-        def squares():
-            for r in range(5):
-                a = slice(r, r + 6, 5) if r < 4 else slice(9, 10)
-                b = slice(r + 1, r + 7, 5) if r < 4 else slice(10, 11)
-                n = 2 if r < 4 else 1
-
-                def square(a=a, b=b, n=n):
-                    nc.vector.scalar_tensor_tensor(out=tmp[:, 0:n], in0=se[:, a], scalar=-2.0, in1=se[:, a], op0=ALU.mult, op1=ALU.mult)
-                    nc.vector.scalar_tensor_tensor(out=se[:, b], in0=se[:, a], scalar=2.0, in1=ce[:, a], op0=ALU.mult, op1=ALU.mult)
-                    nc.vector.tensor_scalar(out=ce[:, b], in0=tmp[:, 0:n], scalar1=1.0, scalar2=None, op0=ALU.add)
-
-                tiny.append(square)
-            tiny.append(lambda: nc.vector.tensor_add(sc[:], ce[:], se[:]))
-
-        def products(n0, w, lo, hi, on_scalar, base=0):
-            for t, tab in ((0, tab_w), (1, tab_u)):
-                if on_scalar:
-                    nc.scalar.activation(out=prod[:, t, base : base + hi - lo], in_=tab[:, lo:hi], func=ACT.Copy, scale=se[:, w : w + 1])
-                else:
-                    nc.vector.tensor_scalar(out=prod[:, t, 0 : hi - lo], in0=tab[:, lo:hi], scalar1=se[:, w : w + 1], scalar2=None, op0=ALU.mult)
-
-        def rotate(which, n0, w, lo, hi, base=0):
-            tab, coef, t, op = (
-                (tab_u, ce, 0, ALU.add),
-                (tab_w, ce, 1, ALU.subtract),
-                (tab_c, sc, 1, ALU.add),
-            )[which]
-            nc.vector.scalar_tensor_tensor(
-                out=tab[:, n0 + lo : n0 + hi], in0=tab[:, lo:hi], scalar=coef[:, w : w + 1], in1=prod[:, t, base : base + hi - lo], op0=ALU.mult, op1=op
-            )
-
-        level_weights = (2, 3, 4, 5, 6, 7, 8, 0, 1)
-
-        def level(k):
-            n = 1 << k
-            tiny.append(lambda: products(n, level_weights[k], 0, n, False))
-
-            def turn_all():
-                for which in range(3):
-                    rotate(which, n, level_weights[k], 0, n)
-
-            tiny.append(turn_all)
 
         wd = keep.tile([P, LAT], I32, name="wd", align_bytes=64)
         wds = keep.tile([P, LAT], U8, name="wds", align_bytes=64)
         wrs = keep.tile([P, 256], U8, name="wrs", align_bytes=64)
         wus = planes[:, 768:1024]
 
-        def permute_weights():
+        def permute_first():
             nc.vector.tensor_copy(out=wd[:].rearrange("p (t m) -> p t m", t=PACK), in_=wd_raw[:].rearrange("p (m t) -> p t m", t=PACK))
             nc.vector.tensor_copy(out=wds[:].rearrange("p (t m) -> p t m", t=PACK), in_=planes[:, 0:512].rearrange("p (m t) -> p t m", t=PACK))
+
+        def permute_second():
             nc.vector.tensor_copy(
                 out=wrs[:].rearrange("p (f h j) -> p f h j", f=2, h=H), in_=planes[:, 512:768].rearrange("p (h f j) -> p f h j", f=2, h=H)
             )
@@ -223,7 +195,7 @@ def tile_multiheadlatentattention_pa_t_w8_kernel(
                 xs_t = mid.tile([P, TILES, E], BF16, name="xs", tag="xs", align_bytes=64)
                 st["xs", g] = xs_t
             xs = st["xs", g]
-            step = 1 if g == 0 else 2
+            step = 1 if g < 2 else 2
             for i in tiles[::step]:
                 nc.vector.tensor_tensor(
                     out=xs[:, i : i + step, :].rearrange("p i k -> p (i k)"),
@@ -277,31 +249,18 @@ def tile_multiheadlatentattention_pa_t_w8_kernel(
                 st["m1", g, t] = bank
 
         def latent(g):
-            dp = mid.tile([P, PACK, SPLIT], BF16, name="dp", tag="dp", align_bytes=64)
-            dw = mid.tile([P, 2, TOK - SPLIT, 2], BF16, name="dw", tag="dw", align_bytes=64)
+            dw = mid.tile([P, 2, TOK, 2], BF16, name="dw", tag="dw", align_bytes=64)
             for t in range(PACK):
-                bank = st["m1", g, t]
-                nc.scalar.activation(out=dw[:, t // 2, :, t % 2], in_=bank[:, SPLIT:TOK], func=ACT.Identity, bias=bias_d[:, t : t + 1])
-                nc.scalar.activation(out=dp[:, t, :], in_=bank[:, 0:SPLIT], func=ACT.Identity, bias=bias_d[:, t : t + 1])
-            st["dp", g] = dp
+                nc.scalar.activation(out=dw[:, t // 2, :, t % 2], in_=st["m1", g, t][:], func=ACT.Identity, bias=bias_d[:, t : t + 1])
             st["dw", g] = dw
 
-        def weave(g):
-            dg = mid.tile([P, TOK, PACK], BF16, name="dg", tag="dg", align_bytes=64)
-            nc.gpsimd.tensor_scalar(
-                out=dg[:, 0:SPLIT, :],
-                in0=st["dp", g][:].rearrange("p t n -> p n t"),
-                scalar1=1.0,
-                scalar2=0.0,
-                op0=ALU.mult,
-                op1=ALU.add,
-            )
-            st["dg", g] = dg
-
-        def weave_high(g):
-            nc.scalar.copy(
-                out=st["dg", g][:, SPLIT:TOK, :].rearrange("p n t -> p (n t)").bitcast(F32).rearrange("p (n u) -> p n u", u=2),
-                in_=st["dw", g][:].rearrange("p u n e -> p (u n e)").bitcast(F32).rearrange("p (u n) -> p n u", u=2),
+        def weave(g, engine, lo, hi):
+            if ("dg", g) not in st:
+                dg_t = mid.tile([P, TOK, PACK], BF16, name="dg", tag="dg", align_bytes=64)
+                st["dg", g] = dg_t
+            engine(
+                out=st["dg", g][:, lo:hi, :].rearrange("p n t -> p (n t)").bitcast(F32).rearrange("p (n u) -> p n u", u=2),
+                in_=st["dw", g][:].rearrange("p u n e -> p (u n e)").bitcast(F32).rearrange("p (u n) -> p n u", u=2)[:, lo:hi, :],
             )
 
         def mm_rope(g, parts):
@@ -338,11 +297,11 @@ def tile_multiheadlatentattention_pa_t_w8_kernel(
         SUM, HI, LO = (0, 1), (1,), (0,)
 
         def rope(g, parts):
-            bias_col, tab = {SUM: (2, tab_c), HI: (1, tab_u), LO: (0, tab_w)}[parts]
+            bias_col, row = {SUM: (2, 0), HI: (1, 1), LO: (0, 2)}[parts]
             c0 = (g // B) * TOK
             kt = mid.tile([P, TOK], F32, name="kt", tag="k%d" % bias_col)
             nc.vector.scalar_tensor_tensor(
-                out=kt[:], in0=st["k", g, parts][:], scalar=bias_r[:, bias_col : bias_col + 1], in1=tab[:, c0 : c0 + TOK], op0=ALU.add, op1=ALU.mult
+                out=kt[:], in0=st["k", g, parts][:], scalar=bias_r[:, bias_col : bias_col + 1], in1=tab[:, row, c0 : c0 + TOK], op0=ALU.add, op1=ALU.mult
             )
             st["kt", g, parts] = kt
 
@@ -380,20 +339,27 @@ def tile_multiheadlatentattention_pa_t_w8_kernel(
         def store(g):
             nc.sync.dma_start(out=out_view[g % B, g // B], in_=st["ot", g][:].rearrange("p i h d -> p (i h d)"))
 
-        for g in (0, 1):
-            for pair in (0, 1):
-                widen(g, (2 * pair, 2 * pair + 1))
-                turn(g, pair)
-                if g == 0:
-                    unturn(g, pair)
-            if g == 0:
-                nc.scalar.copy(out=xscale[:, E : 2 * E], in_=xscale[:, 0:E])
-                permute_weights()
-                columns()
-                squares()
-                for k in range(9):
-                    level(k)
-                drip(2)
+        table_a()
+        widen(0, (0, 1))
+        turn(0, 0)
+        unturn(0, 0)
+        table_b()
+        widen(0, (2, 3))
+        turn(0, 1)
+        unturn(0, 1)
+        permute_first()
+        table_c()
+        columns()
+        nc.scalar.copy(out=xscale[:, E : 2 * E], in_=xscale[:, 0:E])
+        quant("xg", "xq", 0)
+        mm1(0)
+        latent(0)
+        widen(1, (0, 1))
+        turn(1, 0)
+        table_d()
+        permute_second()
+        widen(1, (2, 3))
+        turn(1, 1)
 
         for i in range(GROUPS + 2):
             if i + 4 < GROUPS:
@@ -403,14 +369,7 @@ def tile_multiheadlatentattention_pa_t_w8_kernel(
                 if c + 1 < GROUPS:
                     unturn(c + 1, pair)
             if 0 <= b < GROUPS:
-                weave(b)
-                weave_high(b)
-            if i == 2:
-                products(512, 9, 0, 512, True)
-            if i == 6:
-                products(1024, 10, 0, 512, True, 512)
-            if i == 10:
-                products(1024, 10, 512, 1024, True)
+                weave(b, nc.scalar.copy, SPLIT, TOK)
             if a >= 0:
                 ot_t = outs.tile([P, TILES, H, D], F32, name="ot", tag="ot")
                 st["ot", a] = ot_t
@@ -423,28 +382,21 @@ def tile_multiheadlatentattention_pa_t_w8_kernel(
                 place(a, 0)
                 back(a, 1)
                 place(a, 1)
-            if c < GROUPS:
+            if 0 < c < GROUPS:
                 quant("xg", "xq", c)
                 mm1(c)
                 latent(c)
-            drip(4)
+            if 0 <= b < GROUPS:
+                weave(b, nc.vector.tensor_copy, 0, SPLIT)
             if a >= 0:
                 finish_q1(a, 0)
                 finish_q1(a, 1)
                 store(a)
-            if 3 <= i <= 5:
-                rotate(i - 3, 512, 9, 0, 512)
-            if 7 <= i <= 9:
-                rotate(i - 7, 1024, 10, 0, 512, 512)
-            if 11 <= i <= 13:
-                rotate(i - 11, 1024, 10, 512, 1024)
-            drip(4)
             if 0 <= b < GROUPS:
                 quant("dg", "dq", b)
                 mm_rope(b, SUM)
                 mm_rope(b, HI)
                 mm_rope(b, LO)
             for pair in (0, 1):
-                drip(4)
                 widen(c + 2, (2 * pair, 2 * pair + 1))
                 turn(c + 2, pair)

import math
from contextlib import ExitStack

import concourse.mybir as mybir
from concourse.masks import make_identity

B, S, E, LAT, H = 4, 2048, 512, 512, 4
D = E // H
R = D // 2
HALF = R // 2
FLOPS = 2 * B * S * LAT * (E + 2 * H * R)

F32 = mybir.dt.float32
BF16 = mybir.dt.bfloat16
I32 = mybir.dt.int32
U32 = mybir.dt.uint32
U8 = mybir.dt.uint8
FP8 = mybir.dt.float8_e4m3fn
FP8X4 = mybir.dt.float8_e4m3fn_x4
ALU = mybir.AluOpType
ACT = mybir.ActivationFunctionType

P = 128
PACK = 4
TILES = 4
TOK = P * TILES
QUARTERS = S // TOK
GROUPS = B * QUARTERS
SPLIT = 256
DUMMIES = (0, 1, 0, 1)


def tile_multiheadlatentattention_pa_t_w8_kernel(
    tc, x_bytes, x_scale, wd_words, wd_scales, bq_d, wu_words, wu_scales, bq_u, wr_words, wr_scales, brq, out
):
    nc = tc.nc
    x_view = x_bytes.rearrange("b (c p i) k -> b c p (i k)", p=P, i=TILES)
    out_view = out.rearrange("b (c p i) h d -> b c p (i h d)", p=P, i=TILES)

    with ExitStack() as ctx:
        keep = ctx.enter_context(tc.tile_pool(name="keep", bufs=1))
        xin = ctx.enter_context(tc.tile_pool(name="xin", bufs=5))
        mid = ctx.enter_context(tc.tile_pool(name="mid", bufs=2))
        outs = ctx.enter_context(tc.tile_pool(name="outs", bufs=4))
        psum_v = ctx.enter_context(tc.psum_pool(name="psum_v", bufs=3))
        psum_s = ctx.enter_context(tc.psum_pool(name="psum_s", bufs=5))
        ctx.enter_context(tc.manual_schedule())

        def vbank():
            t = psum_v.tile([P, 512], F32, name="vb", tag="vb")
            return t

        def sbank():
            t = psum_s.tile([P, 512], F32, name="sb", tag="sb")
            return t

        x_tiles = {}

        def warm(bank, n):
            for k in range(n):
                nc.tensor.matmul(bank[:, 0:128], ident[:], ident[:], start=True, stop=True)

        def load(g):
            t = xin.tile([P, TILES * E], U8, name="xb", tag="xb", align_bytes=64)
            nc.sync.dma_start(out=t[:], in_=x_view[g % B, g // B])
            x_tiles[g] = t

        xscale = keep.tile([P, 2 * E], F32, name="xscale")
        nc.scalar.dma_start(out=xscale[:, 0:E], in_=x_scale.rearrange("a b k -> (a b k)").partition_broadcast(P))
        load(0)
        planes = keep.tile([P, 1024], U8, name="planes", align_bytes=64)
        nc.vector.memset(planes[:].bitcast(I32), 0)
        wd_raw = keep.tile([P, LAT], I32, name="wd_raw", align_bytes=64)
        nc.sync.dma_start(out=wd_raw[:], in_=wd_words[0].rearrange("p n t -> p (n t)").bitcast(I32))
        for q in range(4):
            nc.sync.dma_start(out=planes[32 * q : 32 * q + 4, 0:512].bitcast(I32), in_=wd_scales[0, 4 * q : 4 * q + 4, :].bitcast(I32))
        load(1)
        bd_raw = keep.tile([P, PACK], BF16, name="bd_raw")
        nc.sync.dma_start(out=bd_raw[:], in_=bq_d.rearrange("(p t) -> p t", t=PACK))
        br_raw = keep.tile([2, P], BF16, name="br_raw")
        for f in range(2):
            nc.sync.dma_start(
                out=br_raw[f : f + 1, :].rearrange("o (h j) -> o h j", h=H),
                in_=brq.rearrange("(h f j) -> f h j", f=2, j=HALF)[f : f + 1],
            )
        bu = keep.tile([P, H * R], BF16, name="bu")
        nc.sync.dma_start(out=bu[:], in_=bq_u.partition_broadcast(P))
        wr = keep.tile([P, 256], I32, name="wr", align_bytes=64)
        wr_src = wr_words[0].rearrange("p n t -> p (n t)").bitcast(I32).rearrange("p (h f j) -> f p h j", f=2, j=HALF)
        for f in range(2):
            nc.sync.dma_start(out=wr[:, 128 * f : 128 * f + 128].rearrange("p (h j) -> p h j", h=H), in_=wr_src[f])
        wu = keep.tile([P, 256], I32, name="wu", align_bytes=64)
        nc.sync.dma_start(out=wu[:], in_=wu_words[0].rearrange("p n t -> p (n t)").bitcast(I32))
        for q in range(4):
            nc.sync.dma_start(out=planes[32 * q : 32 * q + 4, 512:768].bitcast(I32), in_=wr_scales[0, 4 * q : 4 * q + 4, :].bitcast(I32))
        for q in range(4):
            nc.sync.dma_start(out=planes[32 * q : 32 * q + 4, 768:1024].bitcast(I32), in_=wu_scales[0, 4 * q : 4 * q + 4, :].bitcast(I32))
        load(2)
        load(3)

        ones = keep.tile([P, H], F32, name="ones")
        nc.vector.memset(ones[:], 1.0)
        seed = keep.tile([P, P], F32, name="seed")
        nc.vector.memset(seed[:], 0.0)
        ident = keep.tile([P, P], F32, name="ident")
        make_identity(nc, ident[:])
        pos = keep.tile([P, TOK], F32, name="pos")
        for c in range(QUARTERS):
            nc.gpsimd.iota(
                pos[32 * c : 32 * c + 32, :].rearrange("p (i m) -> p i m", i=TILES),
                pattern=[[1, TILES], [TILES, P]],
                base=TOK * c,
                channel_multiplier=0,
                allow_small_or_imprecise_dtypes=True,
            )
        brow = keep.tile([P, P], F32, name="brow")
        nc.gpsimd.memset(brow[:], 0.0)
        for j in range(HALF):
            turns = 10000.0 ** (-j / HALF) / (2.0 * math.pi)
            dst, src = seed[0:1, j:P:HALF], ones[0:1, :]
            if j < 24:
                nc.vector.tensor_scalar(out=dst, in0=src, scalar1=turns, scalar2=None, op0=ALU.mult)
            else:
                nc.scalar.mul(dst, src, turns)

        freq = keep.tile([P, 1], F32, name="freq")
        bias_r = keep.tile([P, 3], F32, name="bias_r")
        bias_d = keep.tile([P, PACK], F32, name="bias_d")
        angle = keep.tile([P, 2, TOK], F32, name="angle")
        whole = keep.tile([P, 2, TOK], I32, name="whole")
        sine = keep.tile([P, TOK], F32, name="sine")
        trio = keep.tile([P, 3, TOK], F32, name="trio")
        tab = keep.tile([P, 3, S], F32, name="tab")

        def table_a():
            ct = sbank()
            nc.tensor.transpose(ct[:, 0:128], seed[:], ident[:])
            nc.vector.tensor_copy(out=freq[:], in_=ct[:, 0:1])
            warm(ct, 4)
            for q in range(2):
                nc.scalar.activation(out=angle[:, q, :], in_=pos[:], func=ACT.Copy, scale=freq[:], bias=0.25 * q)

        def table_b():
            nc.vector.tensor_copy(out=whole[:].rearrange("p q n -> p (q n)"), in_=angle[:].rearrange("p q n -> p (q n)"))

        def table_c():
            nc.vector.tensor_tensor(
                out=angle[:].rearrange("p q n -> p (q n)"),
                in0=angle[:].rearrange("p q n -> p (q n)"),
                in1=whole[:].rearrange("p q n -> p (q n)"),
                op=ALU.subtract,
            )
            nc.scalar.activation(out=sine[:], in_=angle[:, 0, :], func=ACT.Sin, scale=2.0 * math.pi)
            nc.scalar.activation(out=trio[:, 0, :], in_=angle[:, 1, :], func=ACT.Sin, scale=2.0 * math.pi)

        def table_d():
            nc.vector.scalar_tensor_tensor(out=trio[:, 1, :], in0=trio[:, 0, :], scalar=-1.0, in1=sine[:], op0=ALU.mult, op1=ALU.subtract)
            nc.vector.tensor_tensor(out=trio[:, 2, :], in0=sine[:], in1=trio[:, 0, :], op=ALU.subtract)
            park = out_view[B - 1, QUARTERS - 1][:, 0 : 3 * TOK]
            nc.sync.dma_start(out=park, in_=trio[:].rearrange("p t n -> p (t n)"))
            for c in range(QUARTERS):
                for h in range(H):
                    nc.sync.dma_start(
                        out=tab[32 * h : 32 * h + 32, :, TOK * c : TOK * (c + 1)], in_=park[32 * c : 32 * c + 32, :].rearrange("p (t n) -> p t n", t=3)
                    )

        def columns():
            ct = sbank()
            nc.vector.tensor_copy(out=brow[0:2, :], in_=br_raw[:])
            nc.tensor.transpose(ct[:, 0:128], brow[:], ident[:])
            nc.vector.tensor_copy(out=bias_r[:, 0:2], in_=ct[:, 0:2])
            nc.vector.tensor_add(bias_r[:, 2:3], bias_r[:, 0:1], bias_r[:, 1:2])
            nc.vector.tensor_copy(out=bias_d[:], in_=bd_raw[:])

        wd = keep.tile([P, LAT], I32, name="wd", align_bytes=64)
        wds = keep.tile([P, LAT], U8, name="wds", align_bytes=64)
        wrs = keep.tile([P, 256], U8, name="wrs", align_bytes=64)
        wus = planes[:, 768:1024]

        def permute_first():
            nc.vector.tensor_copy(out=wd[:].rearrange("p (t m) -> p t m", t=PACK), in_=wd_raw[:].rearrange("p (m t) -> p t m", t=PACK))
            nc.vector.tensor_copy(out=wds[:].rearrange("p (t m) -> p t m", t=PACK), in_=planes[:, 0:512].rearrange("p (m t) -> p t m", t=PACK))

        def permute_second():
            nc.vector.tensor_copy(
                out=wrs[:].rearrange("p (f h j) -> p f h j", f=2, h=H), in_=planes[:, 512:768].rearrange("p (h f j) -> p f h j", f=2, h=H)
            )

        st = {}

        def widen(g, tiles):
            if g >= GROUPS:
                return
            if ("xs", g) not in st:
                xs_t = mid.tile([P, TILES, E], BF16, name="xs", tag="xs", align_bytes=64)
                st["xs", g] = xs_t
            xs = st["xs", g]
            step = 1 if g < 2 else 2
            for i in tiles[::step]:
                nc.vector.tensor_tensor(
                    out=xs[:, i : i + step, :].rearrange("p i k -> p (i k)"),
                    in0=x_tiles[g][:, E * i : E * (i + step)].bitcast(FP8),
                    in1=xscale[:, 0 : E * step],
                    op=ALU.mult,
                )

        def turn(g, pair):
            if g >= GROUPS:
                return
            if ("xg", g) not in st:
                xg_t = mid.tile([P, TOK, PACK], BF16, name="xg", tag="xg", align_bytes=64)
                st["xg", g] = xg_t
            bank = sbank()
            warm(bank, DUMMIES[2 + pair])
            for i in (0, 1):
                words = st["xs", g][:, 2 * pair + i, :].bitcast(F32)
                for u in (0, 1):
                    o = 256 * i + 128 * u
                    nc.tensor.transpose(bank[:, o : o + 128], words[:, u:256:2], ident[:])
            st["xt", g, pair] = bank

        def unturn(g, pair):
            if g >= GROUPS:
                return
            nc.scalar.copy(
                out=st["xg", g][:, 256 * pair : 256 * pair + 256, :].rearrange("p n t -> p (n t)").bitcast(F32).rearrange("p (i r u) -> p i r u", i=2, u=2),
                in_=st["xt", g, pair][:].rearrange("p (i u r) -> p i r u", i=2, u=2),
            )

        def quant(src, dst, g):
            codes = mid.tile([P, TOK], U32, name=dst, tag=dst, align_bytes=64)
            scales = mid.tile([P, TOK], U8, name=dst + "s", tag=dst + "s", align_bytes=64)
            nc.vector.quantize_mx(out=codes[:].bitcast(FP8X4), scales=scales[:], in_=st[src, g][:].rearrange("p n t -> p (n t)"))
            st[dst, g] = (codes, scales)

        def mm1(g):
            codes, scales = st["xq", g]
            for t in range(PACK):
                bank = sbank()
                nc.tensor.matmul_mx(
                    out=bank[:],
                    lhsT=wd[:, 128 * t : 128 * t + 128].bitcast(FP8X4),
                    lhsT_scale=wds[:, 128 * t : 128 * t + 128],
                    rhs=codes[:].bitcast(FP8X4),
                    rhs_scale=scales[:],
                    start=True,
                    stop=True,
                )
                st["m1", g, t] = bank

        def latent(g):
            dw = mid.tile([P, 2, TOK, 2], BF16, name="dw", tag="dw", align_bytes=64)
            for t in range(PACK):
                nc.scalar.activation(out=dw[:, t // 2, :, t % 2], in_=st["m1", g, t][:], func=ACT.Identity, bias=bias_d[:, t : t + 1])
            st["dw", g] = dw

        def weave(g, engine, lo, hi):
            if ("dg", g) not in st:
                dg_t = mid.tile([P, TOK, PACK], BF16, name="dg", tag="dg", align_bytes=64)
                st["dg", g] = dg_t
            engine(
                out=st["dg", g][:, lo:hi, :].rearrange("p n t -> p (n t)").bitcast(F32).rearrange("p (n u) -> p n u", u=2),
                in_=st["dw", g][:].rearrange("p u n e -> p (u n e)").bitcast(F32).rearrange("p (u n) -> p n u", u=2)[:, lo:hi, :],
            )

        def mm_rope(g, parts):
            codes, scales = st["dq", g]
            bank = vbank()
            for n, f in enumerate(parts):
                nc.tensor.matmul_mx(
                    out=bank[:],
                    lhsT=wr[:, 128 * f : 128 * f + 128].bitcast(FP8X4),
                    lhsT_scale=wrs[:, 128 * f : 128 * f + 128],
                    rhs=codes[:].bitcast(FP8X4),
                    rhs_scale=scales[:],
                    start=(n == 0),
                    stop=(n == len(parts) - 1),
                )
            st["k", g, parts] = bank

        def mm_q1(g, pair):
            codes, scales = st["dq", g]
            bank = vbank()
            for i in (0, 1):
                c0 = 256 * pair + 128 * i
                nc.tensor.matmul_mx(
                    out=bank[:, 256 * i : 256 * i + 256],
                    lhsT=codes[:, c0 : c0 + 128].bitcast(FP8X4),
                    lhsT_scale=scales[:, c0 : c0 + 128],
                    rhs=wu[:].bitcast(FP8X4),
                    rhs_scale=wus,
                    start=True,
                    stop=True,
                )
            st["q1", g, pair] = bank

        SUM, HI, LO = (0, 1), (1,), (0,)

        def rope(g, parts):
            bias_col, row = {SUM: (2, 0), HI: (1, 1), LO: (0, 2)}[parts]
            c0 = (g // B) * TOK
            kt = mid.tile([P, TOK], F32, name="kt", tag="k%d" % bias_col)
            nc.vector.scalar_tensor_tensor(
                out=kt[:], in0=st["k", g, parts][:], scalar=bias_r[:, bias_col : bias_col + 1], in1=tab[:, row, c0 : c0 + TOK], op0=ALU.add, op1=ALU.mult
            )
            st["kt", g, parts] = kt

        def finish_q1(g, pair):
            nc.vector.tensor_tensor(
                out=st["ot", g][:, 2 * pair : 2 * pair + 2, :, 0:R],
                in0=st["q1", g, pair][:].rearrange("p (i h d) -> p i h d", i=2, h=H),
                in1=bu[:].rearrange("p (o h d) -> p o h d", o=1, h=H).to_broadcast([P, 2, H, R]),
                op=ALU.add,
            )

        def back(g, half):
            bank = sbank()
            pieces = (st["kt", g, SUM], st["kt", g, HI if half == 0 else LO])
            warm(bank, DUMMIES[half])
            for i in range(TILES):
                for n, piece in enumerate(pieces):
                    nc.tensor.matmul(
                        bank[:, 128 * i : 128 * i + 128],
                        piece[:, 128 * i : 128 * i + 128],
                        ident[:],
                        start=(n == 0),
                        stop=(n == len(pieces) - 1),
                        is_transpose=True,
                    )
            st["o", g, half] = bank

        def place(g, half):
            c0 = R + HALF * half
            nc.scalar.copy(
                out=st["ot", g][:, :, :, c0 : c0 + HALF],
                in_=st["o", g, half][:].rearrange("p (i h j) -> p i h j", i=TILES, h=H),
            )

        def store(g):
            nc.sync.dma_start(out=out_view[g % B, g // B], in_=st["ot", g][:].rearrange("p i h d -> p (i h d)"))

        table_a()
        widen(0, (0, 1))
        turn(0, 0)
        unturn(0, 0)
        table_b()
        widen(0, (2, 3))
        turn(0, 1)
        unturn(0, 1)
        permute_first()
        table_c()
        columns()
        nc.scalar.copy(out=xscale[:, E : 2 * E], in_=xscale[:, 0:E])
        quant("xg", "xq", 0)
        mm1(0)
        latent(0)
        widen(1, (0, 1))
        turn(1, 0)
        table_d()
        permute_second()
        widen(1, (2, 3))
        turn(1, 1)

        for i in range(GROUPS + 2):
            if i + 4 < GROUPS:
                load(i + 4)
            a, b, c = i - 2, i - 1, i
            for pair in (0, 1):
                if c + 1 < GROUPS:
                    unturn(c + 1, pair)
            if 0 <= b < GROUPS:
                weave(b, nc.scalar.copy, SPLIT, TOK)
            if a >= 0:
                ot_t = outs.tile([P, TILES, H, D], F32, name="ot", tag="ot")
                st["ot", a] = ot_t
                rope(a, SUM)
                rope(a, HI)
                rope(a, LO)
                mm_q1(a, 0)
                mm_q1(a, 1)
                back(a, 0)
                place(a, 0)
                back(a, 1)
                place(a, 1)
            if 0 < c < GROUPS:
                quant("xg", "xq", c)
                mm1(c)
                latent(c)
            if 0 <= b < GROUPS:
                weave(b, nc.vector.tensor_copy, 0, SPLIT)
            if a >= 0:
                finish_q1(a, 0)
                finish_q1(a, 1)
                store(a)
            if 0 <= b < GROUPS:
                quant("dg", "dq", b)
                mm_rope(b, SUM)
                mm_rope(b, HI)
                mm_rope(b, LO)
            for pair in (0, 1):
                widen(c + 2, (2 * pair, 2 * pair + 1))
                turn(c + 2, pair)
